import numpy as np
import ml_dtypes


def mxq(x, axis, fmt="e4m3"):
    dtype, down = {"e4m3": (ml_dtypes.float8_e4m3fn, 7), "e5m2": (ml_dtypes.float8_e5m2, 14)}[fmt]
    v = np.moveaxis(np.asarray(x, np.float32).astype(ml_dtypes.bfloat16).astype(np.float64), axis, -1)
    blocks = v.reshape(v.shape[:-1] + (-1, 32))
    amax = np.abs(blocks).max(-1, keepdims=True)
    byte = np.maximum(np.where(amax > 0, np.frexp(amax)[1] - 1 + 127, 0) - down, 1)
    scale = np.exp2(byte - 127.0)
    codes = (blocks / scale).astype(np.float32).astype(dtype).astype(np.float64)
    return np.moveaxis((codes * scale).reshape(v.shape), -1, axis)


WIDE = False


def mx_kscale(k):
    if not WIDE:
        return np.ones(k)
    levels = np.array([10, -10, 5, -5, 0])
    a = np.random.permutation(np.resize(levels, k // 512 * 4)).reshape(k // 512, 4)
    idx = np.arange(k)
    return np.exp2(a[idx // 512, idx % 128 // 32])


BF16 = ml_dtypes.bfloat16


def bf(x):
    return np.asarray(x, np.float32).astype(BF16)


def f64(x):
    return np.asarray(x).astype(np.float64)


B, T, D, E, F = 4, 256, 1024, 1024, 4096
EPS = 1e-6


def rms_norm(x, w):
    rms = np.sqrt(np.mean(x * x, axis=-1, keepdims=True) + EPS)
    return x / rms * w


def setup_inputs():
    s = mx_kscale(D)
    return {"x": bf(np.random.standard_normal((B, T, D))),
            "attn_norm_w": bf((1.0 + 0.1 * np.random.standard_normal(D)) * s),
            "wq": bf(np.random.standard_normal((D, E)) * 1.5 / np.sqrt(D) / s[:, None]),
            "bq": bf(np.random.standard_normal(E) * 0.1),
            "wk": bf(np.random.standard_normal((D, E)) * 1.5 / np.sqrt(D) / s[:, None]),
            "bk": bf(np.random.standard_normal(E) * 0.1),
            "wv": bf(np.random.standard_normal((D, E)) / np.sqrt(D) / s[:, None]),
            "bv": bf(np.random.standard_normal(E) * 0.1)}


def reference(x, attn_norm_w, wq, bq, wk, bk, wv, bv):
    xn = mxq(rms_norm(f64(x), f64(attn_norm_w)), 2, "e4m3")
    q = (xn @ mxq(f64(wq), 0, "e4m3")) + f64(bq)
    k = (xn @ mxq(f64(wk), 0, "e4m3")) + f64(bk)
    v = (xn @ mxq(f64(wv), 0, "e4m3")) + f64(bv)
    return q, k, v

@@ -1,0 +1,220 @@
+from contextlib import ExitStack
+
+import concourse.mybir as mybir
+from concourse.masks import make_identity
+
+F32 = mybir.dt.float32
+BF16 = mybir.dt.bfloat16
+I32 = mybir.dt.int32
+U32 = mybir.dt.uint32
+U8 = mybir.dt.uint8
+FP8X4 = mybir.dt.float8_e4m3fn_x4
+ACT = mybir.ActivationFunctionType
+ALU = mybir.AluOpType
+
+P = 128
+PACK = 4
+K_PASS = P * PACK
+TOKENS = 4 * 256
+D = 1024
+E = 1024
+EPS = 1e-6
+PASSES = D // K_PASS
+TOK_TILES = TOKENS // P
+PAIRS = TOK_TILES // 2
+N_TILE = 512
+N_HALVES = E // N_TILE
+WEIGHTS = 3
+TILE_WORDS = PASSES * P
+
+FLOPS = 2 * TOKENS * D * WEIGHTS * E
+
+
+def tile_tinyblock_pa_kernel(
+    tc, x, attn_norm_w, wq, bq, wk, bk, wv, bv, out_0, out_1, out_2
+):
+    nc = tc.nc
+    weights = [wq, wk, wv]
+    x_rows = x.flatten_outer_dims().rearrange("(p i) d -> p i d", i=TOK_TILES)
+    out_rows = [
+        o.flatten_outer_dims().rearrange("(p i) e -> p i e", i=TOK_TILES)
+        for o in (out_0, out_1, out_2)
+    ]
+
+    with ExitStack() as ctx:
+        ctx.enter_context(tc.manual_schedule())
+        keep = ctx.enter_context(tc.tile_pool(name="keep", bufs=1))
+        work = ctx.enter_context(tc.tile_pool(name="work", bufs=4))
+        results = ctx.enter_context(tc.tile_pool(name="results", bufs=6))
+        psum_stage = ctx.enter_context(tc.psum_pool(name="psum_stage", bufs=3))
+        psum_acc = ctx.enter_context(tc.psum_pool(name="psum_acc", bufs=5))
+
+        x_sb = keep.tile([P, TOK_TILES, D], BF16)
+        w_raw = [
+            [keep.tile([P, PACK, E], BF16, name="w_raw_%d_%d" % (w, c)) for c in range(PASSES)]
+            for w in range(WEIGHTS)
+        ]
+        x_codes = keep.tile([P, TOK_TILES * TILE_WORDS], U32, align_bytes=64)
+        x_scales = keep.tile([P, TOK_TILES * TILE_WORDS], U8, align_bytes=64)
+        w_codes = [
+            keep.tile([P, PASSES, E], U32, name="w_codes_%d" % w, align_bytes=64)
+            for w in range(WEIGHTS)
+        ]
+        w_scales = [
+            keep.tile([P, PASSES, E], U8, name="w_scales_%d" % w, align_bytes=64)
+            for w in range(WEIGHTS)
+        ]
+        vec_rows = keep.tile([P, 1 + WEIGHTS, E], BF16)
+        vec_all = keep.tile([P, 1 + WEIGHTS, E], BF16)
+        ones = keep.tile([P, P], BF16)
+        ident = keep.tile([P, P], BF16)
+        eps_col = keep.tile([P, 1], F32)
+        warm = keep.tile([P, 1], F32)
+        sumsq = keep.tile([P, TOK_TILES], F32)
+        rms = keep.tile([P, TOK_TILES], F32)
+        rstd = keep.tile([P, TOK_TILES], F32)
+
+        def load_x(pair):
+            both = slice(2 * pair, 2 * pair + 2)
+            nc.sync.dma_start(out=x_sb[:, both, :], in_=x_rows[:, both, :])
+
+        def load_w(w, c):
+            rows = weights[w][c * K_PASS : (c + 1) * K_PASS, :]
+            nc.sync.dma_start(out=w_raw[w][c][:], in_=rows.rearrange("(t p) n -> p t n", p=P))
+
+        load_x(0)
+        load_x(1)
+        load_w(0, 0)
+        load_x(2)
+        load_x(3)
+        load_w(0, 1)
+        for w in range(1, WEIGHTS):
+            for c in range(PASSES):
+                load_w(w, c)
+
+        nc.vector.memset(eps_col[:], EPS)
+        nc.vector.memset(vec_rows[:].bitcast(I32), 0)
+        nc.vector.memset(ones[:], 1.0)
+        make_identity(nc, ident[:])
+        nc.scalar.activation(out=warm[:], in_=eps_col[:], func=ACT.Sqrt)
+
+        for v, vec in enumerate((attn_norm_w, bq, bk, bv)):
+            nc.scalar.dma_start(out=vec_rows[0:1, v, :], in_=vec.unsqueeze(0))
+        for v in range(1 + WEIGHTS):
+            spread = psum_stage.tile([P, E], BF16, tag="stage")
+            for h in range(N_HALVES):
+                cols = slice(h * N_TILE, (h + 1) * N_TILE)
+                nc.tensor.matmul(
+                    out=spread[:, cols], lhsT=ones[:], rhs=vec_rows[:, v, cols], start=True, stop=True
+                )
+            nc.vector.tensor_copy(out=vec_all[:, v, :], in_=spread[:])
+        gain_all = vec_all[:, 0, :]
+
+        transposed = {}
+        grouped_x = {}
+
+        def statistics(pair):
+            both = slice(2 * pair, 2 * pair + 2)
+            for i in range(2 * pair, 2 * pair + 2):
+                squares = work.tile([P, D], BF16, tag="squares")
+                nc.scalar.activation(
+                    out=squares[:], in_=x_sb[:, i, :], func=ACT.Square, accum_out=sumsq[:, i : i + 1]
+                )
+            nc.scalar.activation(
+                out=rms[:, both], in_=sumsq[:, both], func=ACT.Sqrt, scale=1.0 / D, bias=eps_col[:]
+            )
+
+        def normalise(pair):
+            both = slice(2 * pair, 2 * pair + 2)
+            nc.vector.reciprocal(out=rstd[:, both], in_=rms[:, both])
+            for i in range(2 * pair, 2 * pair + 2):
+                xn = work.tile([P, D], BF16, tag="xn")
+                nc.vector.scalar_tensor_tensor(
+                    out=xn[:],
+                    in0=x_sb[:, i, :],
+                    scalar=rstd[:, i : i + 1],
+                    in1=gain_all,
+                    op0=ALU.mult,
+                    op1=ALU.mult,
+                )
+                xt = psum_stage.tile([P, PASSES, PACK, P], BF16, tag="stage")
+                for c in range(PASSES):
+                    for t in range(PACK):
+                        first = c * K_PASS + t * P
+                        nc.tensor.transpose(xt[:, c, t, :], xn[:, first : first + P], ident[:])
+                transposed[i] = xt
+
+        def leave_psum(pair):
+            grouped = work.tile([P, 2, PASSES, P, PACK], BF16, tag="grouped_x", align_bytes=64)
+            for half in range(2):
+                xt = transposed[2 * pair + half]
+                nc.scalar.copy(out=grouped[:, half], in_=xt[:].rearrange("p c t r -> p c r t"))
+            grouped_x[pair] = grouped
+
+        def quantise_x(pair):
+            words = slice(2 * pair * TILE_WORDS, (2 * pair + 2) * TILE_WORDS)
+            nc.vector.quantize_mx(
+                out=x_codes[:, words].bitcast(FP8X4),
+                scales=x_scales[:, words],
+                in_=grouped_x[pair][:].rearrange("p a c r t -> p (a c r t)"),
+            )
+
+        grouped_w = {}
+
+        def regroup_w(engine_copy, w, c):
+            grouped = work.tile([P, E * PACK], BF16, tag="grouped_w", align_bytes=64)
+            engine_copy(
+                out=grouped[:].rearrange("p (b i t) -> p b t i", i=4, t=PACK),
+                in_=w_raw[w][c][:].rearrange("p t (b i) -> p b t i", i=4),
+            )
+            grouped_w[(w, c)] = grouped
+
+        def quantise_w(w, c):
+            nc.vector.quantize_mx(
+                out=w_codes[w][:, c, :].bitcast(FP8X4),
+                scales=w_scales[w][:, c, :],
+                in_=grouped_w[(w, c)][:],
+            )
+
+        for step in range(PAIRS + 3):
+            if 2 <= step < PAIRS + 2:
+                leave_psum(step - 2)
+            if step < PAIRS:
+                statistics(step)
+            if 1 <= step < PAIRS + 1:
+                normalise(step - 1)
+            if 1 <= step < PASSES + 1:
+                regroup_w(nc.vector.tensor_copy, 0, step - 1)
+            if 3 <= step:
+                quantise_x(step - 3)
+            if 3 <= step < PASSES + 3:
+                quantise_w(0, step - 3)
+
+        for w in range(1, WEIGHTS):
+            for c in range(PASSES):
+                regroup_w(nc.scalar.copy, w, c)
+
+        for w in range(WEIGHTS):
+            if w > 0:
+                for c in range(PASSES):
+                    quantise_w(w, c)
+            for i in range(TOK_TILES):
+                result = results.tile([P, E], F32)
+                for h in range(N_HALVES):
+                    cols = slice(h * N_TILE, (h + 1) * N_TILE)
+                    acc = psum_acc.tile([P, N_TILE], F32)
+                    for c in range(PASSES):
+                        words = slice((i * PASSES + c) * P, (i * PASSES + c + 1) * P)
+                        nc.tensor.matmul_mx(
+                            out=acc[:],
+                            lhsT=x_codes[:, words].bitcast(FP8X4),
+                            lhsT_scale=x_scales[:, words],
+                            rhs=w_codes[w][:, c, cols].bitcast(FP8X4),
+                            rhs_scale=w_scales[w][:, c, cols],
+                            start=(c == 0),
+                            stop=(c == PASSES - 1),
+                        )
+                    nc.vector.tensor_tensor(
+                        out=result[:, cols], in0=acc[:], in1=vec_all[:, 1 + w, cols], op=ALU.add
+                    )
+                nc.sync.dma_start(out=out_rows[w][:, i, :], in_=result[:])

@@ -27,6 +27,8 @@ N_HALVES = E // N_TILE
 WEIGHTS = 3
 TILE_WORDS = PASSES * P
 
+FIRST_SCALAR_ROW = 10
+
 FLOPS = 2 * TOKENS * D * WEIGHTS * E
 
 
@@ -35,6 +37,7 @@ def tile_tinyblock_pa_kernel(
 ):
     nc = tc.nc
     weights = [wq, wk, wv]
+    vectors = [attn_norm_w, bq, bk, bv]
     x_rows = x.flatten_outer_dims().rearrange("(p i) d -> p i d", i=TOK_TILES)
     out_rows = [
         o.flatten_outer_dims().rearrange("(p i) e -> p i e", i=TOK_TILES)
@@ -82,33 +85,36 @@ def tile_tinyblock_pa_kernel(
             rows = weights[w][c * K_PASS : (c + 1) * K_PASS, :]
             nc.sync.dma_start(out=w_raw[w][c][:], in_=rows.rearrange("(t p) n -> p t n", p=P))
 
+        def load_vector(v):
+            nc.vector.memset(vec_rows[:, v, :].bitcast(I32), 0)
+            nc.sync.dma_start(out=vec_rows[0:1, v, :], in_=vectors[v].unsqueeze(0))
+
+        nc.vector.memset(eps_col[:], EPS)
         load_x(0)
+        load_vector(0)
         load_x(1)
         load_w(0, 0)
+        load_w(0, 1)
+        for v in range(1, 1 + WEIGHTS):
+            load_vector(v)
         load_x(2)
         load_x(3)
-        load_w(0, 1)
         for w in range(1, WEIGHTS):
             for c in range(PASSES):
                 load_w(w, c)
 
-        nc.vector.memset(eps_col[:], EPS)
-        nc.vector.memset(vec_rows[:].bitcast(I32), 0)
         nc.vector.memset(ones[:], 1.0)
         make_identity(nc, ident[:])
         nc.scalar.activation(out=warm[:], in_=eps_col[:], func=ACT.Sqrt)
 
-        for v, vec in enumerate((attn_norm_w, bq, bk, bv)):
-            nc.scalar.dma_start(out=vec_rows[0:1, v, :], in_=vec.unsqueeze(0))
-        for v in range(1 + WEIGHTS):
+        def spread_vector(engine_copy, v):
             spread = psum_stage.tile([P, E], BF16, tag="stage")
             for h in range(N_HALVES):
                 cols = slice(h * N_TILE, (h + 1) * N_TILE)
                 nc.tensor.matmul(
                     out=spread[:, cols], lhsT=ones[:], rhs=vec_rows[:, v, cols], start=True, stop=True
                 )
-            nc.vector.tensor_copy(out=vec_all[:, v, :], in_=spread[:])
-        gain_all = vec_all[:, 0, :]
+            engine_copy(out=vec_all[:, v, :], in_=spread[:])
 
         transposed = {}
         grouped_x = {}
@@ -133,7 +139,7 @@ def tile_tinyblock_pa_kernel(
                     out=xn[:],
                     in0=x_sb[:, i, :],
                     scalar=rstd[:, i : i + 1],
-                    in1=gain_all,
+                    in1=vec_all[:, 0, :],
                     op0=ALU.mult,
                     op1=ALU.mult,
                 )
@@ -169,6 +175,18 @@ def tile_tinyblock_pa_kernel(
             )
             grouped_w[(w, c)] = grouped
 
+        def regroup_w_on_gpsimd(w, c):
+            grouped = work.tile([P, E * PACK], BF16, tag="grouped_w", align_bytes=64)
+            nc.gpsimd.tensor_scalar(
+                out=grouped[:].rearrange("p (n t) -> p n t", t=PACK),
+                in0=w_raw[w][c][:].rearrange("p t n -> p n t"),
+                scalar1=1.0,
+                scalar2=0.0,
+                op0=ALU.mult,
+                op1=ALU.add,
+            )
+            grouped_w[(w, c)] = grouped
+
         def quantise_w(w, c):
             nc.vector.quantize_mx(
                 out=w_codes[w][:, c, :].bitcast(FP8X4),
@@ -176,8 +194,9 @@ def tile_tinyblock_pa_kernel(
                 in_=grouped_w[(w, c)][:],
             )
 
-        for step in range(PAIRS + 3):
-            if 2 <= step < PAIRS + 2:
+        spread_vector(nc.vector.tensor_copy, 0)
+        for step in range(PAIRS + 2):
+            if 2 <= step:
                 leave_psum(step - 2)
             if step < PAIRS:
                 statistics(step)
@@ -185,20 +204,24 @@ def tile_tinyblock_pa_kernel(
                 normalise(step - 1)
             if 1 <= step < PASSES + 1:
                 regroup_w(nc.vector.tensor_copy, 0, step - 1)
-            if 3 <= step:
-                quantise_x(step - 3)
             if 3 <= step < PASSES + 3:
                 quantise_w(0, step - 3)
+        spread_vector(nc.vector.tensor_copy, 1)
+        quantise_x(0)
 
-        for w in range(1, WEIGHTS):
-            for c in range(PASSES):
-                regroup_w(nc.scalar.copy, w, c)
+        def store(w, i, result):
+            nc.sync.dma_start(out=out_rows[w][:, i, :], in_=result[:])
 
+        late_store = None
         for w in range(WEIGHTS):
-            if w > 0:
-                for c in range(PASSES):
-                    quantise_w(w, c)
+            if w + 1 < WEIGHTS:
+                regroup_w(nc.scalar.copy, w + 1, 0)
+                regroup_w_on_gpsimd(w + 1, 1)
             for i in range(TOK_TILES):
+                if w == 0 and i % 2 == 0 and i // 2 + 1 < PAIRS:
+                    quantise_x(i // 2 + 1)
+                row = w * TOK_TILES + i
+                by_scalar = row >= FIRST_SCALAR_ROW and (row - FIRST_SCALAR_ROW) % 3 == 0
                 result = results.tile([P, E], F32)
                 for h in range(N_HALVES):
                     cols = slice(h * N_TILE, (h + 1) * N_TILE)
@@ -214,7 +237,24 @@ def tile_tinyblock_pa_kernel(
                             start=(c == 0),
                             stop=(c == PASSES - 1),
                         )
-                    nc.vector.tensor_tensor(
-                        out=result[:, cols], in0=acc[:], in1=vec_all[:, 1 + w, cols], op=ALU.add
-                    )
-                nc.sync.dma_start(out=out_rows[w][:, i, :], in_=result[:])
+                    bias = vec_all[:, 1 + w, cols]
+                    if by_scalar:
+                        nc.scalar.copy(out=result[:, cols], in_=acc[:])
+                        nc.gpsimd.tensor_tensor(
+                            out=result[:, cols], in0=result[:, cols], in1=bias, op=ALU.add
+                        )
+                    else:
+                        nc.vector.tensor_tensor(out=result[:, cols], in0=acc[:], in1=bias, op=ALU.add)
+                if by_scalar:
+                    late_store = (w, i, result)
+                else:
+                    store(w, i, result)
+                    if late_store is not None:
+                        store(*late_store)
+                        late_store = None
+                if w + 1 < WEIGHTS:
+                    if i == 0:
+                        spread_vector(nc.scalar.copy, 2 + w)
+                    c_next = i - (TOK_TILES - 1 - PASSES)
+                    if 0 <= c_next < PASSES:
+                        quantise_w(w + 1, c_next)

@@ -27,9 +27,12 @@ N_HALVES = E // N_TILE
 WEIGHTS = 3
 TILE_WORDS = PASSES * P
 
-FIRST_SCALAR_ROW = 10
+LEAD = 2
 
 FLOPS = 2 * TOKENS * D * WEIGHTS * E
+
+assert PAIRS == 2 * LEAD
+assert PASSES == LEAD
 
 
 def tile_tinyblock_pa_kernel(
@@ -116,6 +119,7 @@ def tile_tinyblock_pa_kernel(
                 )
             engine_copy(out=vec_all[:, v, :], in_=spread[:])
 
+        normed = {}
         transposed = {}
         grouped_x = {}
 
@@ -143,11 +147,15 @@ def tile_tinyblock_pa_kernel(
                     op0=ALU.mult,
                     op1=ALU.mult,
                 )
+                normed[i] = xn
+
+        def transpose(pair):
+            for i in range(2 * pair, 2 * pair + 2):
                 xt = psum_stage.tile([P, PASSES, PACK, P], BF16, tag="stage")
                 for c in range(PASSES):
                     for t in range(PACK):
                         first = c * K_PASS + t * P
-                        nc.tensor.transpose(xt[:, c, t, :], xn[:, first : first + P], ident[:])
+                        nc.tensor.transpose(xt[:, c, t, :], normed[i][:, first : first + P], ident[:])
                 transposed[i] = xt
 
         def leave_psum(pair):
@@ -175,18 +183,6 @@ def tile_tinyblock_pa_kernel(
             )
             grouped_w[(w, c)] = grouped
 
-        def regroup_w_on_gpsimd(w, c):
-            grouped = work.tile([P, E * PACK], BF16, tag="grouped_w", align_bytes=64)
-            nc.gpsimd.tensor_scalar(
-                out=grouped[:].rearrange("p (n t) -> p n t", t=PACK),
-                in0=w_raw[w][c][:].rearrange("p t n -> p n t"),
-                scalar1=1.0,
-                scalar2=0.0,
-                op0=ALU.mult,
-                op1=ALU.add,
-            )
-            grouped_w[(w, c)] = grouped
-
         def quantise_w(w, c):
             nc.vector.quantize_mx(
                 out=w_codes[w][:, c, :].bitcast(FP8X4),
@@ -194,67 +190,56 @@ def tile_tinyblock_pa_kernel(
                 in_=grouped_w[(w, c)][:],
             )
 
-        spread_vector(nc.vector.tensor_copy, 0)
-        for step in range(PAIRS + 2):
-            if 2 <= step:
-                leave_psum(step - 2)
-            if step < PAIRS:
-                statistics(step)
-            if 1 <= step < PAIRS + 1:
-                normalise(step - 1)
-            if 1 <= step < PASSES + 1:
-                regroup_w(nc.vector.tensor_copy, 0, step - 1)
-            if 3 <= step < PASSES + 3:
-                quantise_w(0, step - 3)
-        spread_vector(nc.vector.tensor_copy, 1)
-        quantise_x(0)
-
-        def store(w, i, result):
+        def project(w, i):
+            result = results.tile([P, E], F32)
+            for h in range(N_HALVES):
+                cols = slice(h * N_TILE, (h + 1) * N_TILE)
+                acc = psum_acc.tile([P, N_TILE], F32)
+                for c in range(PASSES):
+                    words = slice((i * PASSES + c) * P, (i * PASSES + c + 1) * P)
+                    nc.tensor.matmul_mx(
+                        out=acc[:],
+                        lhsT=x_codes[:, words].bitcast(FP8X4),
+                        lhsT_scale=x_scales[:, words],
+                        rhs=w_codes[w][:, c, cols].bitcast(FP8X4),
+                        rhs_scale=w_scales[w][:, c, cols],
+                        start=(c == 0),
+                        stop=(c == PASSES - 1),
+                    )
+                nc.vector.tensor_tensor(
+                    out=result[:, cols], in0=acc[:], in1=vec_all[:, 1 + w, cols], op=ALU.add
+                )
             nc.sync.dma_start(out=out_rows[w][:, i, :], in_=result[:])
 
-        late_store = None
+        spread_vector(nc.vector.tensor_copy, 0)
+        for pair in range(LEAD):
+            statistics(pair)
+        for pair in range(LEAD):
+            normalise(pair)
+            transpose(pair)
+            regroup_w(nc.vector.tensor_copy, 0, pair)
+            leave_psum(pair)
+            statistics(pair + LEAD)
+        quantise_w(0, 0)
+        quantise_x(0)
+        quantise_w(0, 1)
+        spread_vector(nc.vector.tensor_copy, 1)
+
         for w in range(WEIGHTS):
-            if w + 1 < WEIGHTS:
-                regroup_w(nc.scalar.copy, w + 1, 0)
-                regroup_w_on_gpsimd(w + 1, 1)
-            for i in range(TOK_TILES):
-                if w == 0 and i % 2 == 0 and i // 2 + 1 < PAIRS:
-                    quantise_x(i // 2 + 1)
-                row = w * TOK_TILES + i
-                by_scalar = row >= FIRST_SCALAR_ROW and (row - FIRST_SCALAR_ROW) % 3 == 0
-                result = results.tile([P, E], F32)
-                for h in range(N_HALVES):
-                    cols = slice(h * N_TILE, (h + 1) * N_TILE)
-                    acc = psum_acc.tile([P, N_TILE], F32)
-                    for c in range(PASSES):
-                        words = slice((i * PASSES + c) * P, (i * PASSES + c + 1) * P)
-                        nc.tensor.matmul_mx(
-                            out=acc[:],
-                            lhsT=x_codes[:, words].bitcast(FP8X4),
-                            lhsT_scale=x_scales[:, words],
-                            rhs=w_codes[w][:, c, cols].bitcast(FP8X4),
-                            rhs_scale=w_scales[w][:, c, cols],
-                            start=(c == 0),
-                            stop=(c == PASSES - 1),
-                        )
-                    bias = vec_all[:, 1 + w, cols]
-                    if by_scalar:
-                        nc.scalar.copy(out=result[:, cols], in_=acc[:])
-                        nc.gpsimd.tensor_tensor(
-                            out=result[:, cols], in0=result[:, cols], in1=bias, op=ALU.add
-                        )
-                    else:
-                        nc.vector.tensor_tensor(out=result[:, cols], in0=acc[:], in1=bias, op=ALU.add)
-                if by_scalar:
-                    late_store = (w, i, result)
-                else:
-                    store(w, i, result)
-                    if late_store is not None:
-                        store(*late_store)
-                        late_store = None
+            for pair in range(PAIRS):
+                if w == 0 and pair + LEAD < PAIRS:
+                    normalise(pair + LEAD)
                 if w + 1 < WEIGHTS:
-                    if i == 0:
-                        spread_vector(nc.scalar.copy, 2 + w)
-                    c_next = i - (TOK_TILES - 1 - PASSES)
-                    if 0 <= c_next < PASSES:
-                        quantise_w(w + 1, c_next)
+                    if pair < PASSES:
+                        regroup_w(nc.scalar.copy, w + 1, pair)
+                    if pair >= PAIRS - PASSES:
+                        quantise_w(w + 1, pair - (PAIRS - PASSES))
+                project(w, 2 * pair)
+                project(w, 2 * pair + 1)
+                if w == 0 and pair + LEAD < PAIRS:
+                    transpose(pair + LEAD)
+                    leave_psum(pair + LEAD)
+                if w == 0 and pair + 1 < PAIRS:
+                    quantise_x(pair + 1)
+                if w + 1 < WEIGHTS and pair == PASSES:
+                    spread_vector(nc.scalar.copy, 2 + w)

@@ -27,12 +27,9 @@ N_HALVES = E // N_TILE
 WEIGHTS = 3
 TILE_WORDS = PASSES * P
 
-LEAD = 2
+FIRST_SCALAR_ROW = 13
 
 FLOPS = 2 * TOKENS * D * WEIGHTS * E
-
-assert PAIRS == 2 * LEAD
-assert PASSES == LEAD
 
 
 def tile_tinyblock_pa_kernel(
@@ -119,7 +116,6 @@ def tile_tinyblock_pa_kernel(
                 )
             engine_copy(out=vec_all[:, v, :], in_=spread[:])
 
-        normed = {}
         transposed = {}
         grouped_x = {}
 
@@ -147,15 +143,11 @@ def tile_tinyblock_pa_kernel(
                     op0=ALU.mult,
                     op1=ALU.mult,
                 )
-                normed[i] = xn
-
-        def transpose(pair):
-            for i in range(2 * pair, 2 * pair + 2):
                 xt = psum_stage.tile([P, PASSES, PACK, P], BF16, tag="stage")
                 for c in range(PASSES):
                     for t in range(PACK):
                         first = c * K_PASS + t * P
-                        nc.tensor.transpose(xt[:, c, t, :], normed[i][:, first : first + P], ident[:])
+                        nc.tensor.transpose(xt[:, c, t, :], xn[:, first : first + P], ident[:])
                 transposed[i] = xt
 
         def leave_psum(pair):
@@ -190,56 +182,67 @@ def tile_tinyblock_pa_kernel(
                 in_=grouped_w[(w, c)][:],
             )
 
-        def project(w, i):
-            result = results.tile([P, E], F32)
-            for h in range(N_HALVES):
-                cols = slice(h * N_TILE, (h + 1) * N_TILE)
-                acc = psum_acc.tile([P, N_TILE], F32)
-                for c in range(PASSES):
-                    words = slice((i * PASSES + c) * P, (i * PASSES + c + 1) * P)
-                    nc.tensor.matmul_mx(
-                        out=acc[:],
-                        lhsT=x_codes[:, words].bitcast(FP8X4),
-                        lhsT_scale=x_scales[:, words],
-                        rhs=w_codes[w][:, c, cols].bitcast(FP8X4),
-                        rhs_scale=w_scales[w][:, c, cols],
-                        start=(c == 0),
-                        stop=(c == PASSES - 1),
-                    )
-                nc.vector.tensor_tensor(
-                    out=result[:, cols], in0=acc[:], in1=vec_all[:, 1 + w, cols], op=ALU.add
-                )
+        spread_vector(nc.vector.tensor_copy, 0)
+        for step in range(PAIRS + 2):
+            if 2 <= step:
+                leave_psum(step - 2)
+            if step < PAIRS:
+                statistics(step)
+            if 1 <= step < PAIRS + 1:
+                normalise(step - 1)
+            if 1 <= step < PASSES + 1:
+                regroup_w(nc.vector.tensor_copy, 0, step - 1)
+            if 3 <= step < PASSES + 3:
+                quantise_w(0, step - 3)
+        spread_vector(nc.vector.tensor_copy, 1)
+        quantise_x(0)
+
+        def store(w, i, result):
             nc.sync.dma_start(out=out_rows[w][:, i, :], in_=result[:])
 
-        spread_vector(nc.vector.tensor_copy, 0)
-        for pair in range(LEAD):
-            statistics(pair)
-        for pair in range(LEAD):
-            normalise(pair)
-            transpose(pair)
-            regroup_w(nc.vector.tensor_copy, 0, pair)
-            leave_psum(pair)
-            statistics(pair + LEAD)
-        quantise_w(0, 0)
-        quantise_x(0)
-        quantise_w(0, 1)
-        spread_vector(nc.vector.tensor_copy, 1)
-
+        late_store = None
         for w in range(WEIGHTS):
-            for pair in range(PAIRS):
-                if w == 0 and pair + LEAD < PAIRS:
-                    normalise(pair + LEAD)
+            if w + 1 < WEIGHTS:
+                for c in range(PASSES):
+                    regroup_w(nc.scalar.copy, w + 1, c)
+            for i in range(TOK_TILES):
+                if w == 0 and i % 2 == 0 and i // 2 + 1 < PAIRS:
+                    quantise_x(i // 2 + 1)
+                row = w * TOK_TILES + i
+                by_scalar = row >= FIRST_SCALAR_ROW and (row - FIRST_SCALAR_ROW) % 3 == 0
+                result = results.tile([P, E], F32)
+                for h in range(N_HALVES):
+                    cols = slice(h * N_TILE, (h + 1) * N_TILE)
+                    acc = psum_acc.tile([P, N_TILE], F32)
+                    for c in range(PASSES):
+                        words = slice((i * PASSES + c) * P, (i * PASSES + c + 1) * P)
+                        nc.tensor.matmul_mx(
+                            out=acc[:],
+                            lhsT=x_codes[:, words].bitcast(FP8X4),
+                            lhsT_scale=x_scales[:, words],
+                            rhs=w_codes[w][:, c, cols].bitcast(FP8X4),
+                            rhs_scale=w_scales[w][:, c, cols],
+                            start=(c == 0),
+                            stop=(c == PASSES - 1),
+                        )
+                    bias = vec_all[:, 1 + w, cols]
+                    if by_scalar:
+                        nc.scalar.copy(out=result[:, cols], in_=acc[:])
+                        nc.gpsimd.tensor_tensor(
+                            out=result[:, cols], in0=result[:, cols], in1=bias, op=ALU.add
+                        )
+                    else:
+                        nc.vector.tensor_tensor(out=result[:, cols], in0=acc[:], in1=bias, op=ALU.add)
+                if by_scalar:
+                    late_store = (w, i, result)
+                else:
+                    store(w, i, result)
+                    if late_store is not None:
+                        store(*late_store)
+                        late_store = None
                 if w + 1 < WEIGHTS:
-                    if pair < PASSES:
-                        regroup_w(nc.scalar.copy, w + 1, pair)
-                    if pair >= PAIRS - PASSES:
-                        quantise_w(w + 1, pair - (PAIRS - PASSES))
-                project(w, 2 * pair)
-                project(w, 2 * pair + 1)
-                if w == 0 and pair + LEAD < PAIRS:
-                    transpose(pair + LEAD)
-                    leave_psum(pair + LEAD)
-                if w == 0 and pair + 1 < PAIRS:
-                    quantise_x(pair + 1)
-                if w + 1 < WEIGHTS and pair == PASSES:
-                    spread_vector(nc.scalar.copy, 2 + w)
+                    if i == 0:
+                        spread_vector(nc.scalar.copy, 2 + w)
+                    c_next = i - (TOK_TILES - 1 - PASSES)
+                    if 0 <= c_next < PASSES:
+                        quantise_w(w + 1, c_next)

from contextlib import ExitStack

import concourse.mybir as mybir
from concourse.masks import make_identity

F32 = mybir.dt.float32
BF16 = mybir.dt.bfloat16
I32 = mybir.dt.int32
U32 = mybir.dt.uint32
U8 = mybir.dt.uint8
FP8X4 = mybir.dt.float8_e4m3fn_x4
ACT = mybir.ActivationFunctionType
ALU = mybir.AluOpType

P = 128
PACK = 4
K_PASS = P * PACK
TOKENS = 4 * 256
D = 1024
E = 1024
EPS = 1e-6
PASSES = D // K_PASS
TOK_TILES = TOKENS // P
PAIRS = TOK_TILES // 2
N_TILE = 512
N_HALVES = E // N_TILE
WEIGHTS = 3
TILE_WORDS = PASSES * P

FIRST_SCALAR_ROW = 13

FLOPS = 2 * TOKENS * D * WEIGHTS * E


def tile_tinyblock_pa_kernel(
    tc, x, attn_norm_w, wq, bq, wk, bk, wv, bv, out_0, out_1, out_2
):
    nc = tc.nc
    weights = [wq, wk, wv]
    vectors = [attn_norm_w, bq, bk, bv]
    x_rows = x.flatten_outer_dims().rearrange("(p i) d -> p i d", i=TOK_TILES)
    out_rows = [
        o.flatten_outer_dims().rearrange("(p i) e -> p i e", i=TOK_TILES)
        for o in (out_0, out_1, out_2)
    ]

    with ExitStack() as ctx:
        ctx.enter_context(tc.manual_schedule())
        keep = ctx.enter_context(tc.tile_pool(name="keep", bufs=1))
        work = ctx.enter_context(tc.tile_pool(name="work", bufs=4))
        results = ctx.enter_context(tc.tile_pool(name="results", bufs=6))
        psum_stage = ctx.enter_context(tc.psum_pool(name="psum_stage", bufs=3))
        psum_acc = ctx.enter_context(tc.psum_pool(name="psum_acc", bufs=5))

        x_sb = keep.tile([P, TOK_TILES, D], BF16)
        w_raw = [
            [keep.tile([P, PACK, E], BF16, name="w_raw_%d_%d" % (w, c)) for c in range(PASSES)]
            for w in range(WEIGHTS)
        ]
        x_codes = keep.tile([P, TOK_TILES * TILE_WORDS], U32, align_bytes=64)
        x_scales = keep.tile([P, TOK_TILES * TILE_WORDS], U8, align_bytes=64)
        w_codes = [
            keep.tile([P, PASSES, E], U32, name="w_codes_%d" % w, align_bytes=64)
            for w in range(WEIGHTS)
        ]
        w_scales = [
            keep.tile([P, PASSES, E], U8, name="w_scales_%d" % w, align_bytes=64)
            for w in range(WEIGHTS)
        ]
        vec_rows = keep.tile([P, 1 + WEIGHTS, E], BF16)
        vec_all = keep.tile([P, 1 + WEIGHTS, E], BF16)
        ones = keep.tile([P, P], BF16)
        ident = keep.tile([P, P], BF16)
        eps_col = keep.tile([P, 1], F32)
        warm = keep.tile([P, 1], F32)
        sumsq = keep.tile([P, TOK_TILES], F32)
        rms = keep.tile([P, TOK_TILES], F32)
        rstd = keep.tile([P, TOK_TILES], F32)

        def load_x(pair):
            both = slice(2 * pair, 2 * pair + 2)
            nc.sync.dma_start(out=x_sb[:, both, :], in_=x_rows[:, both, :])

        def load_w(w, c):
            rows = weights[w][c * K_PASS : (c + 1) * K_PASS, :]
            nc.sync.dma_start(out=w_raw[w][c][:], in_=rows.rearrange("(t p) n -> p t n", p=P))

        def load_vector(v):
            nc.vector.memset(vec_rows[:, v, :].bitcast(I32), 0)
            nc.sync.dma_start(out=vec_rows[0:1, v, :], in_=vectors[v].unsqueeze(0))

        nc.vector.memset(eps_col[:], EPS)
        load_x(0)
        load_vector(0)
        load_x(1)
        load_w(0, 0)
        load_w(0, 1)
        for v in range(1, 1 + WEIGHTS):
            load_vector(v)
        load_x(2)
        load_x(3)
        for w in range(1, WEIGHTS):
            for c in range(PASSES):
                load_w(w, c)

        nc.vector.memset(ones[:], 1.0)
        make_identity(nc, ident[:])
        nc.scalar.activation(out=warm[:], in_=eps_col[:], func=ACT.Sqrt)

        def spread_vector(engine_copy, v):
            spread = psum_stage.tile([P, E], BF16, tag="stage")
            for h in range(N_HALVES):
                cols = slice(h * N_TILE, (h + 1) * N_TILE)
                nc.tensor.matmul(
                    out=spread[:, cols], lhsT=ones[:], rhs=vec_rows[:, v, cols], start=True, stop=True
                )
            engine_copy(out=vec_all[:, v, :], in_=spread[:])

        transposed = {}
        grouped_x = {}

        def statistics(pair):
            both = slice(2 * pair, 2 * pair + 2)
            for i in range(2 * pair, 2 * pair + 2):
                squares = work.tile([P, D], BF16, tag="squares")
                nc.scalar.activation(
                    out=squares[:], in_=x_sb[:, i, :], func=ACT.Square, accum_out=sumsq[:, i : i + 1]
                )
            nc.scalar.activation(
                out=rms[:, both], in_=sumsq[:, both], func=ACT.Sqrt, scale=1.0 / D, bias=eps_col[:]
            )

        def normalise(pair):
            both = slice(2 * pair, 2 * pair + 2)
            nc.vector.reciprocal(out=rstd[:, both], in_=rms[:, both])
            for i in range(2 * pair, 2 * pair + 2):
                xn = work.tile([P, D], BF16, tag="xn")
                nc.vector.scalar_tensor_tensor(
                    out=xn[:],
                    in0=x_sb[:, i, :],
                    scalar=rstd[:, i : i + 1],
                    in1=vec_all[:, 0, :],
                    op0=ALU.mult,
                    op1=ALU.mult,
                )
                xt = psum_stage.tile([P, PASSES, PACK, P], BF16, tag="stage")
                for c in range(PASSES):
                    for t in range(PACK):
                        first = c * K_PASS + t * P
                        nc.tensor.transpose(xt[:, c, t, :], xn[:, first : first + P], ident[:])
                transposed[i] = xt

        def leave_psum(pair):
            grouped = work.tile([P, 2, PASSES, P, PACK], BF16, tag="grouped_x", align_bytes=64)
            for half in range(2):
                xt = transposed[2 * pair + half]
                nc.scalar.copy(out=grouped[:, half], in_=xt[:].rearrange("p c t r -> p c r t"))
            grouped_x[pair] = grouped

        def quantise_x(pair):
            words = slice(2 * pair * TILE_WORDS, (2 * pair + 2) * TILE_WORDS)
            nc.vector.quantize_mx(
                out=x_codes[:, words].bitcast(FP8X4),
                scales=x_scales[:, words],
                in_=grouped_x[pair][:].rearrange("p a c r t -> p (a c r t)"),
            )

        grouped_w = {}

        def regroup_w(engine_copy, w, c):
            grouped = work.tile([P, E * PACK], BF16, tag="grouped_w", align_bytes=64)
            engine_copy(
                out=grouped[:].rearrange("p (b i t) -> p b t i", i=4, t=PACK),
                in_=w_raw[w][c][:].rearrange("p t (b i) -> p b t i", i=4),
            )
            grouped_w[(w, c)] = grouped

        def quantise_w(w, c):
            nc.vector.quantize_mx(
                out=w_codes[w][:, c, :].bitcast(FP8X4),
                scales=w_scales[w][:, c, :],
                in_=grouped_w[(w, c)][:],
            )

        spread_vector(nc.vector.tensor_copy, 0)
        for step in range(PAIRS + 2):
            if 2 <= step:
                leave_psum(step - 2)
            if step < PAIRS:
                statistics(step)
            if 1 <= step < PAIRS + 1:
                normalise(step - 1)
            if 1 <= step < PASSES + 1:
                regroup_w(nc.vector.tensor_copy, 0, step - 1)
            if 3 <= step < PASSES + 3:
                quantise_w(0, step - 3)
        spread_vector(nc.vector.tensor_copy, 1)
        quantise_x(0)

        def store(w, i, result):
            nc.sync.dma_start(out=out_rows[w][:, i, :], in_=result[:])

        late_store = None
        for w in range(WEIGHTS):
            if w + 1 < WEIGHTS:
                for c in range(PASSES):
                    regroup_w(nc.scalar.copy, w + 1, c)
            for i in range(TOK_TILES):
                if w == 0 and i % 2 == 0 and i // 2 + 1 < PAIRS:
                    quantise_x(i // 2 + 1)
                row = w * TOK_TILES + i
                by_scalar = row >= FIRST_SCALAR_ROW and (row - FIRST_SCALAR_ROW) % 3 == 0
                result = results.tile([P, E], F32)
                for h in range(N_HALVES):
                    cols = slice(h * N_TILE, (h + 1) * N_TILE)
                    acc = psum_acc.tile([P, N_TILE], F32)
                    for c in range(PASSES):
                        words = slice((i * PASSES + c) * P, (i * PASSES + c + 1) * P)
                        nc.tensor.matmul_mx(
                            out=acc[:],
                            lhsT=x_codes[:, words].bitcast(FP8X4),
                            lhsT_scale=x_scales[:, words],
                            rhs=w_codes[w][:, c, cols].bitcast(FP8X4),
                            rhs_scale=w_scales[w][:, c, cols],
                            start=(c == 0),
                            stop=(c == PASSES - 1),
                        )
                    bias = vec_all[:, 1 + w, cols]
                    if by_scalar:
                        nc.scalar.copy(out=result[:, cols], in_=acc[:])
                        nc.gpsimd.tensor_tensor(
                            out=result[:, cols], in0=result[:, cols], in1=bias, op=ALU.add
                        )
                    else:
                        nc.vector.tensor_tensor(out=result[:, cols], in0=acc[:], in1=bias, op=ALU.add)
                if by_scalar:
                    late_store = (w, i, result)
                else:
                    store(w, i, result)
                    if late_store is not None:
                        store(*late_store)
                        late_store = None
                if w + 1 < WEIGHTS:
                    if i == 0:
                        spread_vector(nc.scalar.copy, 2 + w)
                    c_next = i - (TOK_TILES - 1 - PASSES)
                    if 0 <= c_next < PASSES:
                        quantise_w(w + 1, c_next)
